import numpy as np
import ml_dtypes


def mxq(x, axis, fmt="e4m3"):
    dtype, down = {"e4m3": (ml_dtypes.float8_e4m3fn, 7), "e5m2": (ml_dtypes.float8_e5m2, 14)}[fmt]
    v = np.moveaxis(np.asarray(x, np.float32).astype(ml_dtypes.bfloat16).astype(np.float64), axis, -1)
    blocks = v.reshape(v.shape[:-1] + (-1, 32))
    amax = np.abs(blocks).max(-1, keepdims=True)
    byte = np.maximum(np.where(amax > 0, np.frexp(amax)[1] - 1 + 127, 0) - down, 1)
    scale = np.exp2(byte - 127.0)
    codes = (blocks / scale).astype(np.float32).astype(dtype).astype(np.float64)
    return np.moveaxis((codes * scale).reshape(v.shape), -1, axis)


WIDE = False


def mx_kscale(k):
    if not WIDE:
        return np.ones(k)
    levels = np.array([10, -10, 5, -5, 0])
    a = np.random.permutation(np.resize(levels, k // 512 * 4)).reshape(k // 512, 4)
    idx = np.arange(k)
    return np.exp2(a[idx // 512, idx % 128 // 32])


BF16 = ml_dtypes.bfloat16


def bf(x):
    return np.asarray(x, np.float32).astype(BF16)


def f64(x):
    return np.asarray(x).astype(np.float64)


B, S, D, H, DH, L, R = 8, 512, 2048, 4, 128, 2048, 64
DV = L - L // 2


def setup_inputs():
    u = mx_kscale(DV)
    return {"q_rot": bf(np.random.standard_normal((B, S, H, DH))),
            "k_rot": bf(np.random.standard_normal((B, S, H, DH))),
            "c_v": bf(np.random.standard_normal((B, S, DV)) * u),
            "W_v_dec": bf(np.random.standard_normal((DV, H * DH)) * 3.0 / np.sqrt(DV) / u[:, None])}


def reference(q_rot, k_rot, c_v, W_v_dec):
    v = (mxq(f64(c_v), 2, "e4m3") @ mxq(f64(W_v_dec), 0, "e4m3")).reshape(B, S, H, DH)
    sc = f64(q_rot).transpose(0, 2, 1, 3) @ f64(k_rot).transpose(0, 2, 3, 1) * (1.0 / np.sqrt(DH))
    e = np.exp(sc - sc.max(-1, keepdims=True))
    ctx = (mxq(e, 3, "e4m3") @ mxq(v.transpose(0, 2, 1, 3), 2, "e4m3")) / e.sum(-1, keepdims=True)
    return ctx.transpose(0, 2, 1, 3).reshape(B, S, H * DH)

@@ -1,0 +1,282 @@
+from contextlib import ExitStack
+import math
+
+import concourse.mybir as mybir
+from concourse.masks import make_identity
+
+B, S, H, DH, DV = 8, 512, 4, 128, 1024
+FLOPS = 2 * B * S * DV * H * DH + 2 * 2 * B * H * S * S * DH
+
+BF16 = mybir.dt.bfloat16
+F32 = mybir.dt.float32
+U32 = mybir.dt.uint32
+U8 = mybir.dt.uint8
+FP8X4 = mybir.dt.float8_e4m3fn_x4
+EXP = mybir.ActivationFunctionType.Exp
+MULT = mybir.AluOpType.mult
+FREE_AXIS = mybir.AxisListType.X
+
+P = 128
+PACK = 4
+TILES = S // P
+L_PASSES = DV // (P * PACK)
+HEADS = B * H
+SCALE = 1.0 / math.sqrt(DH)
+
+QK_LEAD = 2
+SCORE_LEAD = 1
+VALUE_LEAD = 1
+LATENT_LEAD = VALUE_LEAD + TILES
+CONTEXT_LAG = 1
+
+assert TILES == PACK
+assert B * PACK == HEADS
+
+
+def tile_multiheadlatentattention_pb_t_kernel(tc, q_rot, k_rot, c_v, W_v_dec, out):
+    nc = tc.nc
+    with ExitStack() as stack:
+        loads = stack.enter_context(tc.tile_pool(name="loads", bufs=1))
+        consts = stack.enter_context(tc.tile_pool(name="consts", bufs=1))
+        pair = stack.enter_context(tc.tile_pool(name="pair", bufs=2))
+        qk_pool = stack.enter_context(tc.tile_pool(name="qk_pool", bufs=QK_LEAD + 1))
+        e_pool = stack.enter_context(tc.tile_pool(name="e_pool", bufs=2 * TILES))
+        stats = stack.enter_context(tc.tile_pool(name="stats", bufs=4))
+        score_banks = stack.enter_context(tc.psum_pool(name="score_banks", bufs=TILES))
+        work_banks = stack.enter_context(tc.psum_pool(name="work_banks", bufs=4))
+
+        w_raw = consts.tile([P, L_PASSES, PACK, H * DH], BF16)
+        nc.sync.dma_start(
+            out=w_raw[:].rearrange("p g (u e) n -> p (g u) (e n)", u=2, e=2),
+            in_=W_v_dec.rearrange("(a p e) n -> p a (e n)", p=P, e=2),
+        )
+        cv_sb, q_sb, k_sb = [], [], []
+        for b in range(B):
+            cv_b = loads.tile([P, PACK, DV], BF16, name="cv_sb%d" % b)
+            nc.sync.dma_start(out=cv_b[:], in_=c_v[b].rearrange("(p t) l -> p t l", t=PACK))
+            q_b = loads.tile([P, TILES, H * DH], BF16, name="q_sb%d" % b)
+            nc.sync.dma_start(out=q_b[:], in_=q_rot[b].rearrange("(p j) h d -> p j (h d)", j=TILES))
+            k_b = loads.tile([P, PACK, H * DH], BF16, name="k_sb%d" % b)
+            nc.sync.dma_start(out=k_b[:], in_=k_rot[b].rearrange("(p t) h d -> p t (h d)", t=PACK))
+            cv_sb.append(cv_b)
+            q_sb.append(q_b)
+            k_sb.append(k_b)
+
+        ident_bf = consts.tile([P, P], BF16)
+        make_identity(nc, ident_bf[:])
+        ident_f32 = consts.tile([P, P], F32)
+        make_identity(nc, ident_f32[:])
+
+        w_grouped = consts.tile([P, L_PASSES, H * DH, PACK], BF16, align_bytes=64)
+        for g in range(L_PASSES):
+            nc.vector.tensor_copy(out=w_grouped[:, g], in_=w_raw[:, g].rearrange("p t n -> p n t"))
+        w_codes = consts.tile([P, L_PASSES, H * DH], U32, align_bytes=64)
+        w_scales = consts.tile([P, L_PASSES, H * DH], U8, align_bytes=64)
+        nc.vector.quantize_mx(
+            out=w_codes[:].rearrange("p g n -> p (g n)").bitcast(FP8X4),
+            scales=w_scales[:].rearrange("p g n -> p (g n)"),
+            in_=w_grouped[:].rearrange("p g n t -> p (g n t)"),
+        )
+
+        cvT_ps, cv_grouped, cv_codes, cv_scales = {}, {}, {}, {}
+        v_ps, v_grouped, v_codes, v_scales = {}, {}, {}, {}
+        qkT_ps, qkT = {}, {}
+        score_ps, row_max, neg_bias, row_sum = {}, {}, {}, {}
+        e_rows, eT_ps, e_grouped, e_codes, e_scales = {}, {}, {}, {}, {}
+        ctx_ps = {}
+
+        def latent_transposes(i):
+            b, t = divmod(i, PACK)
+            words = cv_sb[b][:, t, :].bitcast(F32)
+            bank = work_banks.tile([P, L_PASSES, 2, P], F32, tag="work")
+            for g in range(L_PASSES):
+                for u in range(2):
+                    first = (2 * g + u) * P
+                    nc.tensor.transpose(bank[:, g, u, :], words[:, first : first + P], ident_f32[:])
+            cvT_ps[i] = bank
+
+        def regroup_latent(i):
+            cv_group = pair.tile([P, L_PASSES * P * PACK], BF16, align_bytes=64)
+            nc.vector.tensor_copy(
+                out=cv_group[:].bitcast(F32).rearrange("p (g s u) -> p g s u", g=L_PASSES, u=2),
+                in_=cvT_ps[i][:].rearrange("p g u s -> p g s u"),
+            )
+            cv_grouped[i] = cv_group
+
+        def quantise_latent(i):
+            b, t = divmod(i, PACK)
+            if t == 0:
+                cv_code = pair.tile([P, PACK, L_PASSES * P], U32, align_bytes=64)
+                cv_scale = pair.tile([P, PACK, L_PASSES * P], U8, align_bytes=64)
+                cv_codes[b], cv_scales[b] = cv_code, cv_scale
+            nc.vector.quantize_mx(
+                out=cv_codes[b][:, t, :].bitcast(FP8X4),
+                scales=cv_scales[b][:, t, :],
+                in_=cv_grouped[i][:],
+            )
+
+        def value_passes(i):
+            b, h = divmod(i, H)
+            head_cols = slice(h * DH, (h + 1) * DH)
+            bank = work_banks.tile([P, PACK, DH], F32, tag="work")
+            for t in range(PACK):
+                for g in range(L_PASSES):
+                    key_cols = slice(g * P, (g + 1) * P)
+                    nc.tensor.matmul_mx(
+                        out=bank[:, t, :],
+                        lhsT=cv_codes[b][:, t, key_cols].bitcast(FP8X4),
+                        lhsT_scale=cv_scales[b][:, t, key_cols],
+                        rhs=w_codes[:, g, head_cols].bitcast(FP8X4),
+                        rhs_scale=w_scales[:, g, head_cols],
+                        start=(g == 0),
+                        stop=(g == L_PASSES - 1),
+                    )
+            v_ps[i] = bank
+
+        def regroup_values(i):
+            v_group = pair.tile([P, DH, PACK], BF16, align_bytes=64)
+            nc.vector.tensor_copy(out=v_group[:], in_=v_ps[i][:].rearrange("p t d -> p d t"))
+            v_grouped[i] = v_group
+
+        def quantise_values(i):
+            b, h = divmod(i, H)
+            if h == 0:
+                v_code = pair.tile([P, H, DH], U32, align_bytes=64)
+                v_scale = pair.tile([P, H, DH], U8, align_bytes=64)
+                v_codes[b], v_scales[b] = v_code, v_scale
+            nc.vector.quantize_mx(
+                out=v_codes[b][:, h, :].bitcast(FP8X4),
+                scales=v_scales[b][:, h, :],
+                in_=v_grouped[i][:].rearrange("p d t -> p (d t)"),
+            )
+
+        def qk_transposes(i):
+            b, h = divmod(i, H)
+            head_cols = slice(h * DH, (h + 1) * DH)
+            bank = work_banks.tile([P, 2, TILES, P], BF16, tag="work")
+            for j in range(TILES):
+                nc.tensor.transpose(bank[:, 0, j, :], q_sb[b][:, j, head_cols], ident_bf[:])
+            for t in range(PACK):
+                nc.tensor.transpose(bank[:, 1, t, :], k_sb[b][:, t, head_cols], ident_bf[:])
+            qkT_ps[i] = bank
+
+        def copy_qk(i):
+            both = qk_pool.tile([P, 2, S], BF16)
+            nc.scalar.copy(out=both[:], in_=qkT_ps[i][:].rearrange("p a j s -> p a (j s)"))
+            qkT[i] = both
+
+        def score_tile(i, j):
+            if j == 0:
+                maxima = stats.tile([P, TILES], F32)
+                row_max[i] = maxima
+            bank = score_banks.tile([P, S], F32)
+            nc.tensor.matmul(
+                bank[:], lhsT=qkT[i][:, 0, j * P : (j + 1) * P], rhs=qkT[i][:, 1, :], start=True, stop=True
+            )
+            nc.vector.reduce_max(out=row_max[i][:, j : j + 1], in_=bank[:], axis=FREE_AXIS)
+            score_ps[i, j] = bank
+
+        def softmax_bias(i):
+            bias = stats.tile([P, TILES], F32)
+            nc.vector.tensor_scalar_mul(out=bias[:], in0=row_max[i][:], scalar1=-SCALE)
+            neg_bias[i] = bias
+
+        def exponentials(i):
+            sums = stats.tile([P, TILES], F32)
+            for j in range(TILES):
+                e_tile = e_pool.tile([P, S], BF16)
+                nc.scalar.activation(
+                    out=e_tile[:],
+                    in_=score_ps[i, j][:],
+                    func=EXP,
+                    bias=neg_bias[i][:, j : j + 1],
+                    scale=SCALE,
+                    accum_out=sums[:, j : j + 1],
+                )
+                e_rows[i, j] = e_tile
+            row_sum[i] = sums
+
+        def e_transposes(i, j):
+            if j % 2 == 0:
+                bank = work_banks.tile([P, 2, PACK, P], BF16, tag="work")
+                eT_ps[i, j // 2] = bank
+            for t in range(PACK):
+                nc.tensor.transpose(
+                    eT_ps[i, j // 2][:, j % 2, t, :], e_rows[i, j][:, t * P : (t + 1) * P], ident_bf[:]
+                )
+
+        def regroup_e(i):
+            e_group = pair.tile([P, TILES, P, PACK], BF16, align_bytes=64)
+            for half in range(TILES // 2):
+                nc.scalar.copy(
+                    out=e_group[:, 2 * half : 2 * half + 2],
+                    in_=eT_ps[i, half][:].rearrange("p j t q -> p j q t"),
+                )
+            e_grouped[i] = e_group
+
+        def quantise_e(i):
+            e_code = pair.tile([P, S], U32, align_bytes=64)
+            e_scale = pair.tile([P, S], U8, align_bytes=64)
+            nc.vector.quantize_mx(
+                out=e_code[:].bitcast(FP8X4),
+                scales=e_scale[:],
+                in_=e_grouped[i][:].rearrange("p j q t -> p (j q t)"),
+            )
+            e_codes[i], e_scales[i] = e_code, e_scale
+
+        def context_passes(i):
+            b, h = divmod(i, H)
+            bank = work_banks.tile([P, TILES, DH], F32, tag="work")
+            for j in range(TILES):
+                query_cols = slice(j * P, (j + 1) * P)
+                nc.tensor.matmul_mx(
+                    out=bank[:, j, :],
+                    lhsT=e_codes[i][:, query_cols].bitcast(FP8X4),
+                    lhsT_scale=e_scales[i][:, query_cols],
+                    rhs=v_codes[b][:, h, :].bitcast(FP8X4),
+                    rhs_scale=v_scales[b][:, h, :],
+                    start=True,
+                    stop=True,
+                )
+            ctx_ps[i] = bank
+
+        def normalise_and_store(i):
+            b, h = divmod(i, H)
+            inv_sum = stats.tile([P, TILES], F32)
+            nc.vector.reciprocal(out=inv_sum[:], in_=row_sum[i][:])
+            result = pair.tile([P, TILES, DH], F32)
+            nc.vector.tensor_tensor(
+                out=result[:],
+                in0=ctx_ps[i][:],
+                in1=inv_sum[:].unsqueeze(2).to_broadcast([P, TILES, DH]),
+                op=MULT,
+            )
+            nc.sync.dma_start(
+                out=out[b].rearrange("(p j) n -> p j n", j=TILES)[:, :, h * DH : (h + 1) * DH],
+                in_=result[:],
+            )
+
+        def run(stage, i):
+            if 0 <= i < HEADS:
+                stage(i)
+
+        for r in range(-LATENT_LEAD, HEADS + CONTEXT_LAG):
+            for j in range(TILES):
+                if 0 <= r + SCORE_LEAD < HEADS:
+                    score_tile(r + SCORE_LEAD, j)
+                if 0 <= r < HEADS:
+                    e_transposes(r, j)
+            run(softmax_bias, r + SCORE_LEAD)
+            run(context_passes, r - CONTEXT_LAG)
+            run(value_passes, r + VALUE_LEAD)
+            run(latent_transposes, r + LATENT_LEAD)
+            run(qk_transposes, r + QK_LEAD)
+            run(regroup_e, r)
+            run(copy_qk, r + QK_LEAD)
+            run(exponentials, r + SCORE_LEAD)
+            run(normalise_and_store, r - CONTEXT_LAG)
+            run(regroup_values, r + VALUE_LEAD)
+            run(regroup_latent, r + LATENT_LEAD)
+            run(quantise_values, r + VALUE_LEAD)
+            run(quantise_latent, r + LATENT_LEAD)
+            run(quantise_e, r)

@@ -14,20 +14,23 @@ U8 = mybir.dt.uint8
 FP8X4 = mybir.dt.float8_e4m3fn_x4
 EXP = mybir.ActivationFunctionType.Exp
 MULT = mybir.AluOpType.mult
-FREE_AXIS = mybir.AxisListType.X
+ADD = mybir.AluOpType.add
+MIN = mybir.AluOpType.min
 
 P = 128
 PACK = 4
 TILES = S // P
 L_PASSES = DV // (P * PACK)
 HEADS = B * H
+UNITS = HEADS * TILES
 SCALE = 1.0 / math.sqrt(DH)
 
-QK_LEAD = 2
-SCORE_LEAD = 1
-VALUE_LEAD = 1
+QK_LEAD = 3
+VALUE_LEAD = 2
 LATENT_LEAD = VALUE_LEAD + TILES
-CONTEXT_LAG = 1
+QUANTISE_LAG = 1
+CONTEXT_LAG = 2
+STORE_LAG = 3
 
 assert TILES == PACK
 assert B * PACK == HEADS
@@ -38,12 +41,13 @@ def tile_multiheadlatentattention_pb_t_kernel(tc, q_rot, k_rot, c_v, W_v_dec, ou
     with ExitStack() as stack:
         loads = stack.enter_context(tc.tile_pool(name="loads", bufs=1))
         consts = stack.enter_context(tc.tile_pool(name="consts", bufs=1))
-        pair = stack.enter_context(tc.tile_pool(name="pair", bufs=2))
-        qk_pool = stack.enter_context(tc.tile_pool(name="qk_pool", bufs=QK_LEAD + 1))
-        e_pool = stack.enter_context(tc.tile_pool(name="e_pool", bufs=2 * TILES))
-        stats = stack.enter_context(tc.tile_pool(name="stats", bufs=4))
-        score_banks = stack.enter_context(tc.psum_pool(name="score_banks", bufs=TILES))
-        work_banks = stack.enter_context(tc.psum_pool(name="work_banks", bufs=4))
+        two = stack.enter_context(tc.tile_pool(name="two", bufs=2))
+        three = stack.enter_context(tc.tile_pool(name="three", bufs=3))
+        four = stack.enter_context(tc.tile_pool(name="four", bufs=4))
+        six = stack.enter_context(tc.tile_pool(name="six", bufs=6))
+        score_banks = stack.enter_context(tc.psum_pool(name="score_banks", bufs=3))
+        eT_banks = stack.enter_context(tc.psum_pool(name="eT_banks", bufs=2))
+        side_banks = stack.enter_context(tc.psum_pool(name="side_banks", bufs=3))
 
         w_raw = consts.tile([P, L_PASSES, PACK, H * DH], BF16)
         nc.sync.dma_start(
@@ -78,26 +82,86 @@ def tile_multiheadlatentattention_pb_t_kernel(tc, q_rot, k_rot, c_v, W_v_dec, ou
             in_=w_grouped[:].rearrange("p g n t -> p (g n t)"),
         )
 
+        score_ps, z_sb, neg_max, e_rows, eT_ps, eT_sb = {}, {}, {}, {}, {}, {}
+        row_sum, inv_sum, e_grouped, e_codes, e_scales, ctx_ps = {}, {}, {}, {}, {}, {}
         cvT_ps, cv_grouped, cv_codes, cv_scales = {}, {}, {}, {}
         v_ps, v_grouped, v_codes, v_scales = {}, {}, {}, {}
         qkT_ps, qkT = {}, {}
-        score_ps, row_max, neg_bias, row_sum = {}, {}, {}, {}
-        e_rows, eT_ps, e_grouped, e_codes, e_scales = {}, {}, {}, {}, {}
-        ctx_ps = {}
+
+        def scores(u):
+            i, j = divmod(u, TILES)
+            score_bank = score_banks.tile([P, S], F32)
+            nc.tensor.matmul(
+                score_bank[:],
+                lhsT=qkT[i][:, 0, j * P : (j + 1) * P],
+                rhs=qkT[i][:, 1, :],
+                start=True,
+                stop=True,
+            )
+            score_ps[u] = score_bank
+
+        def scale_and_min(u):
+            z = four.tile([P, S], F32)
+            z_min = six.tile([P, 1], F32)
+            nc.vector.tensor_scalar(
+                out=z[:], in0=score_ps[u][:], scalar1=-SCALE, scalar2=None, op0=MULT, op1=MIN, accum_out=z_min[:]
+            )
+            z_sb[u], neg_max[u] = z, z_min
+
+        def exponential(u):
+            i, j = divmod(u, TILES)
+            if j == 0:
+                sums = six.tile([P, TILES], F32)
+                row_sum[i] = sums
+            e_tile = four.tile([P, S], BF16)
+            nc.scalar.activation(
+                out=e_tile[:],
+                in_=z_sb[u][:],
+                func=EXP,
+                bias=neg_max[u][:],
+                scale=-1.0,
+                accum_out=row_sum[i][:, j : j + 1],
+            )
+            e_rows[u] = e_tile
+
+        def e_transposes(u):
+            eT_bank = eT_banks.tile([P, PACK, P], BF16)
+            for t in range(PACK):
+                nc.tensor.transpose(eT_bank[:, t, :], e_rows[u][:, t * P : (t + 1) * P], ident_bf[:])
+            eT_ps[u] = eT_bank
+
+        def copy_eT(u):
+            eT_tile = four.tile([P, PACK, P], BF16)
+            nc.scalar.copy(out=eT_tile[:], in_=eT_ps[u][:])
+            eT_sb[u] = eT_tile
+
+        def regroup_e(u):
+            i, j = divmod(u, TILES)
+            if j == 0:
+                e_group = three.tile([P, TILES, P, PACK], BF16, align_bytes=64)
+                e_grouped[i] = e_group
+            nc.gpsimd.tensor_scalar(
+                out=e_grouped[i][:, j],
+                in0=eT_sb[u][:].rearrange("p t q -> p q t"),
+                scalar1=1.0,
+                scalar2=0.0,
+                op0=MULT,
+                op1=ADD,
+            )
 
         def latent_transposes(i):
             b, t = divmod(i, PACK)
             words = cv_sb[b][:, t, :].bitcast(F32)
-            bank = work_banks.tile([P, L_PASSES, 2, P], F32, tag="work")
+            cvT_bank = side_banks.tile([P, L_PASSES, 2, P], F32, tag="side")
             for g in range(L_PASSES):
                 for u in range(2):
                     first = (2 * g + u) * P
-                    nc.tensor.transpose(bank[:, g, u, :], words[:, first : first + P], ident_f32[:])
-            cvT_ps[i] = bank
+                    nc.tensor.transpose(cvT_bank[:, g, u, :], words[:, first : first + P], ident_f32[:])
+            cvT_ps[i] = cvT_bank
 
         def regroup_latent(i):
-            cv_group = pair.tile([P, L_PASSES * P * PACK], BF16, align_bytes=64)
-            nc.vector.tensor_copy(
+            cv_group = two.tile([P, L_PASSES * P * PACK], BF16, align_bytes=64)
+            nc.scalar.copy(
                 out=cv_group[:].bitcast(F32).rearrange("p (g s u) -> p g s u", g=L_PASSES, u=2),
                 in_=cvT_ps[i][:].rearrange("p g u s -> p g s u"),
             )
@@ -106,8 +170,8 @@ def tile_multiheadlatentattention_pb_t_kernel(tc, q_rot, k_rot, c_v, W_v_dec, ou
         def quantise_latent(i):
             b, t = divmod(i, PACK)
             if t == 0:
-                cv_code = pair.tile([P, PACK, L_PASSES * P], U32, align_bytes=64)
-                cv_scale = pair.tile([P, PACK, L_PASSES * P], U8, align_bytes=64)
+                cv_code = two.tile([P, PACK, L_PASSES * P], U32, align_bytes=64)
+                cv_scale = two.tile([P, PACK, L_PASSES * P], U8, align_bytes=64)
                 cv_codes[b], cv_scales[b] = cv_code, cv_scale
             nc.vector.quantize_mx(
                 out=cv_codes[b][:, t, :].bitcast(FP8X4),
@@ -118,12 +182,12 @@ def tile_multiheadlatentattention_pb_t_kernel(tc, q_rot, k_rot, c_v, W_v_dec, ou
         def value_passes(i):
             b, h = divmod(i, H)
             head_cols = slice(h * DH, (h + 1) * DH)
-            bank = work_banks.tile([P, PACK, DH], F32, tag="work")
+            v_bank = side_banks.tile([P, PACK, DH], F32, tag="side")
             for t in range(PACK):
                 for g in range(L_PASSES):
                     key_cols = slice(g * P, (g + 1) * P)
                     nc.tensor.matmul_mx(
-                        out=bank[:, t, :],
+                        out=v_bank[:, t, :],
                         lhsT=cv_codes[b][:, t, key_cols].bitcast(FP8X4),
                         lhsT_scale=cv_scales[b][:, t, key_cols],
                         rhs=w_codes[:, g, head_cols].bitcast(FP8X4),
@@ -131,18 +195,18 @@ def tile_multiheadlatentattention_pb_t_kernel(tc, q_rot, k_rot, c_v, W_v_dec, ou
                         start=(g == 0),
                         stop=(g == L_PASSES - 1),
                     )
-            v_ps[i] = bank
+            v_ps[i] = v_bank
 
         def regroup_values(i):
-            v_group = pair.tile([P, DH, PACK], BF16, align_bytes=64)
+            v_group = two.tile([P, DH, PACK], BF16, align_bytes=64)
             nc.vector.tensor_copy(out=v_group[:], in_=v_ps[i][:].rearrange("p t d -> p d t"))
             v_grouped[i] = v_group
 
         def quantise_values(i):
             b, h = divmod(i, H)
             if h == 0:
-                v_code = pair.tile([P, H, DH], U32, align_bytes=64)
-                v_scale = pair.tile([P, H, DH], U8, align_bytes=64)
+                v_code = two.tile([P, H, DH], U32, align_bytes=64)
+                v_scale = two.tile([P, H, DH], U8, align_bytes=64)
                 v_codes[b], v_scales[b] = v_code, v_scale
             nc.vector.quantize_mx(
                 out=v_codes[b][:, h, :].bitcast(FP8X4),
@@ -153,70 +217,21 @@ def tile_multiheadlatentattention_pb_t_kernel(tc, q_rot, k_rot, c_v, W_v_dec, ou
         def qk_transposes(i):
             b, h = divmod(i, H)
             head_cols = slice(h * DH, (h + 1) * DH)
-            bank = work_banks.tile([P, 2, TILES, P], BF16, tag="work")
+            qkT_bank = side_banks.tile([P, 2, TILES, P], BF16, tag="side")
             for j in range(TILES):
-                nc.tensor.transpose(bank[:, 0, j, :], q_sb[b][:, j, head_cols], ident_bf[:])
+                nc.tensor.transpose(qkT_bank[:, 0, j, :], q_sb[b][:, j, head_cols], ident_bf[:])
             for t in range(PACK):
-                nc.tensor.transpose(bank[:, 1, t, :], k_sb[b][:, t, head_cols], ident_bf[:])
-            qkT_ps[i] = bank
+                nc.tensor.transpose(qkT_bank[:, 1, t, :], k_sb[b][:, t, head_cols], ident_bf[:])
+            qkT_ps[i] = qkT_bank
 
         def copy_qk(i):
-            both = qk_pool.tile([P, 2, S], BF16)
-            nc.scalar.copy(out=both[:], in_=qkT_ps[i][:].rearrange("p a j s -> p a (j s)"))
-            qkT[i] = both
-
-        def score_tile(i, j):
-            if j == 0:
-                maxima = stats.tile([P, TILES], F32)
-                row_max[i] = maxima
-            bank = score_banks.tile([P, S], F32)
-            nc.tensor.matmul(
-                bank[:], lhsT=qkT[i][:, 0, j * P : (j + 1) * P], rhs=qkT[i][:, 1, :], start=True, stop=True
-            )
-            nc.vector.reduce_max(out=row_max[i][:, j : j + 1], in_=bank[:], axis=FREE_AXIS)
-            score_ps[i, j] = bank
-
-        def softmax_bias(i):
-            bias = stats.tile([P, TILES], F32)
-            nc.vector.tensor_scalar_mul(out=bias[:], in0=row_max[i][:], scalar1=-SCALE)
-            neg_bias[i] = bias
-
-        def exponentials(i):
-            sums = stats.tile([P, TILES], F32)
-            for j in range(TILES):
-                e_tile = e_pool.tile([P, S], BF16)
-                nc.scalar.activation(
-                    out=e_tile[:],
-                    in_=score_ps[i, j][:],
-                    func=EXP,
-                    bias=neg_bias[i][:, j : j + 1],
-                    scale=SCALE,
-                    accum_out=sums[:, j : j + 1],
-                )
-                e_rows[i, j] = e_tile
-            row_sum[i] = sums
-
-        def e_transposes(i, j):
-            if j % 2 == 0:
-                bank = work_banks.tile([P, 2, PACK, P], BF16, tag="work")
-                eT_ps[i, j // 2] = bank
-            for t in range(PACK):
-                nc.tensor.transpose(
-                    eT_ps[i, j // 2][:, j % 2, t, :], e_rows[i, j][:, t * P : (t + 1) * P], ident_bf[:]
-                )
-
-        def regroup_e(i):
-            e_group = pair.tile([P, TILES, P, PACK], BF16, align_bytes=64)
-            for half in range(TILES // 2):
-                nc.scalar.copy(
-                    out=e_group[:, 2 * half : 2 * half + 2],
-                    in_=eT_ps[i, half][:].rearrange("p j t q -> p j q t"),
-                )
-            e_grouped[i] = e_group
+            qkT_tile = six.tile([P, 2, S], BF16)
+            nc.scalar.copy(out=qkT_tile[:], in_=qkT_ps[i][:].rearrange("p a j s -> p a (j s)"))
+            qkT[i] = qkT_tile
 
         def quantise_e(i):
-            e_code = pair.tile([P, S], U32, align_bytes=64)
-            e_scale = pair.tile([P, S], U8, align_bytes=64)
+            e_code = three.tile([P, S], U32, align_bytes=64)
+            e_scale = three.tile([P, S], U8, align_bytes=64)
             nc.vector.quantize_mx(
                 out=e_code[:].bitcast(FP8X4),
                 scales=e_scale[:],
@@ -224,13 +239,18 @@ def tile_multiheadlatentattention_pb_t_kernel(tc, q_rot, k_rot, c_v, W_v_dec, ou
             )
             e_codes[i], e_scales[i] = e_code, e_scale
 
+        def invert_sums(i):
+            inverse = three.tile([P, TILES], F32)
+            nc.vector.reciprocal(out=inverse[:], in_=row_sum[i][:])
+            inv_sum[i] = inverse
+
         def context_passes(i):
             b, h = divmod(i, H)
-            bank = work_banks.tile([P, TILES, DH], F32, tag="work")
+            ctx_bank = side_banks.tile([P, TILES, DH], F32, tag="side")
             for j in range(TILES):
                 query_cols = slice(j * P, (j + 1) * P)
                 nc.tensor.matmul_mx(
-                    out=bank[:, j, :],
+                    out=ctx_bank[:, j, :],
                     lhsT=e_codes[i][:, query_cols].bitcast(FP8X4),
                     lhsT_scale=e_scales[i][:, query_cols],
                     rhs=v_codes[b][:, h, :].bitcast(FP8X4),
@@ -238,17 +258,15 @@ def tile_multiheadlatentattention_pb_t_kernel(tc, q_rot, k_rot, c_v, W_v_dec, ou
                     start=True,
                     stop=True,
                 )
-            ctx_ps[i] = bank
+            ctx_ps[i] = ctx_bank
 
         def normalise_and_store(i):
             b, h = divmod(i, H)
-            inv_sum = stats.tile([P, TILES], F32)
-            nc.vector.reciprocal(out=inv_sum[:], in_=row_sum[i][:])
-            result = pair.tile([P, TILES, DH], F32)
+            result = three.tile([P, TILES, DH], F32)
             nc.vector.tensor_tensor(
                 out=result[:],
                 in0=ctx_ps[i][:],
-                in1=inv_sum[:].unsqueeze(2).to_broadcast([P, TILES, DH]),
+                in1=inv_sum[i][:].unsqueeze(2).to_broadcast([P, TILES, DH]),
                 op=MULT,
             )
             nc.sync.dma_start(
@@ -256,27 +274,40 @@ def tile_multiheadlatentattention_pb_t_kernel(tc, q_rot, k_rot, c_v, W_v_dec, ou
                 in_=result[:],
             )
 
-        def run(stage, i):
-            if 0 <= i < HEADS:
-                stage(i)
+        def unit_step(step, u):
+            if 0 <= u < UNITS:
+                step(u)
 
-        for r in range(-LATENT_LEAD, HEADS + CONTEXT_LAG):
-            for j in range(TILES):
-                if 0 <= r + SCORE_LEAD < HEADS:
-                    score_tile(r + SCORE_LEAD, j)
-                if 0 <= r < HEADS:
-                    e_transposes(r, j)
-            run(softmax_bias, r + SCORE_LEAD)
-            run(context_passes, r - CONTEXT_LAG)
-            run(value_passes, r + VALUE_LEAD)
-            run(latent_transposes, r + LATENT_LEAD)
-            run(qk_transposes, r + QK_LEAD)
-            run(regroup_e, r)
-            run(copy_qk, r + QK_LEAD)
-            run(exponentials, r + SCORE_LEAD)
-            run(normalise_and_store, r - CONTEXT_LAG)
-            run(regroup_values, r + VALUE_LEAD)
-            run(regroup_latent, r + LATENT_LEAD)
-            run(quantise_values, r + VALUE_LEAD)
-            run(quantise_latent, r + LATENT_LEAD)
-            run(quantise_e, r)
+        def side_job(job, i):
+            if 0 <= i < HEADS:
+                job(i)
+
+        def beat(u):
+            unit_step(scores, u + 3)
+            unit_step(e_transposes, u)
+            unit_step(scale_and_min, u + 2)
+            unit_step(exponential, u + 1)
+            unit_step(copy_eT, u - 1)
+            unit_step(regroup_e, u - 2)
+
+        stack.enter_context(tc.manual_schedule())
+        for r in range(-LATENT_LEAD, HEADS + STORE_LAG):
+            beat(TILES * r)
+            side_job(latent_transposes, r + LATENT_LEAD)
+            side_job(normalise_and_store, r - STORE_LAG)
+
+            beat(TILES * r + 1)
+            side_job(qk_transposes, r + QK_LEAD)
+            side_job(regroup_latent, r + LATENT_LEAD)
+            side_job(quantise_values, r + VALUE_LEAD - 1)
+            side_job(invert_sums, r - CONTEXT_LAG)
+
+            beat(TILES * r + 2)
+            side_job(value_passes, r + VALUE_LEAD)
+            side_job(copy_qk, r + QK_LEAD)
+            side_job(quantise_latent, r + LATENT_LEAD)
+            side_job(quantise_e, r - QUANTISE_LAG)
+
+            beat(TILES * r + 3)
+            side_job(context_passes, r - CONTEXT_LAG)
+            side_job(regroup_values, r + VALUE_LEAD)

@@ -290,7 +290,6 @@ def tile_multiheadlatentattention_pb_t_kernel(tc, q_rot, k_rot, c_v, W_v_dec, ou
             unit_step(copy_eT, u - 1)
             unit_step(regroup_e, u - 2)
 
-        stack.enter_context(tc.manual_schedule())
         for r in range(-LATENT_LEAD, HEADS + STORE_LAG):
             beat(TILES * r)
             side_job(latent_transposes, r + LATENT_LEAD)

@@ -25,9 +25,8 @@ HEADS = B * H
 UNITS = HEADS * TILES
 SCALE = 1.0 / math.sqrt(DH)
 
-QK_LEAD = 3
-VALUE_LEAD = 2
-LATENT_LEAD = VALUE_LEAD + TILES
+QK_LEAD = 2
+LATENT_LEAD = TILES
 QUANTISE_LAG = 1
 CONTEXT_LAG = 2
 STORE_LAG = 3
@@ -225,7 +224,7 @@ def tile_multiheadlatentattention_pb_t_kernel(tc, q_rot, k_rot, c_v, W_v_dec, ou
             qkT_ps[i] = qkT_bank
 
         def copy_qk(i):
-            qkT_tile = six.tile([P, 2, S], BF16)
+            qkT_tile = four.tile([P, 2, S], BF16)
             nc.scalar.copy(out=qkT_tile[:], in_=qkT_ps[i][:].rearrange("p a j s -> p a (j s)"))
             qkT[i] = qkT_tile
 
@@ -290,6 +289,7 @@ def tile_multiheadlatentattention_pb_t_kernel(tc, q_rot, k_rot, c_v, W_v_dec, ou
             unit_step(copy_eT, u - 1)
             unit_step(regroup_e, u - 2)
 
+        stack.enter_context(tc.manual_schedule())
         for r in range(-LATENT_LEAD, HEADS + STORE_LAG):
             beat(TILES * r)
             side_job(latent_transposes, r + LATENT_LEAD)
@@ -298,15 +298,15 @@ def tile_multiheadlatentattention_pb_t_kernel(tc, q_rot, k_rot, c_v, W_v_dec, ou
             beat(TILES * r + 1)
             side_job(qk_transposes, r + QK_LEAD)
             side_job(regroup_latent, r + LATENT_LEAD)
-            side_job(quantise_values, r + VALUE_LEAD - 1)
+            side_job(regroup_values, r - QUANTISE_LAG)
             side_job(invert_sums, r - CONTEXT_LAG)
 
             beat(TILES * r + 2)
-            side_job(value_passes, r + VALUE_LEAD)
             side_job(copy_qk, r + QK_LEAD)
             side_job(quantise_latent, r + LATENT_LEAD)
             side_job(quantise_e, r - QUANTISE_LAG)
 
             beat(TILES * r + 3)
             side_job(context_passes, r - CONTEXT_LAG)
-            side_job(regroup_values, r + VALUE_LEAD)
+            side_job(value_passes, r)
+            side_job(quantise_values, r - QUANTISE_LAG)

@@ -14,7 +14,6 @@ U8 = mybir.dt.uint8
 FP8X4 = mybir.dt.float8_e4m3fn_x4
 EXP = mybir.ActivationFunctionType.Exp
 MULT = mybir.AluOpType.mult
-ADD = mybir.AluOpType.add
 MIN = mybir.AluOpType.min
 
 P = 128
@@ -56,11 +55,11 @@ def tile_multiheadlatentattention_pb_t_kernel(tc, q_rot, k_rot, c_v, W_v_dec, ou
         cv_sb, q_sb, k_sb = [], [], []
         for b in range(B):
             cv_b = loads.tile([P, PACK, DV], BF16, name="cv_sb%d" % b)
-            nc.sync.dma_start(out=cv_b[:], in_=c_v[b].rearrange("(p t) l -> p t l", t=PACK))
+            nc.sync.dma_start(out=cv_b[:].rearrange("p (u e) l -> p u (e l)", u=2), in_=c_v[b].rearrange("(u p e) l -> p u (e l)", u=2, e=2))
             q_b = loads.tile([P, TILES, H * DH], BF16, name="q_sb%d" % b)
             nc.sync.dma_start(out=q_b[:], in_=q_rot[b].rearrange("(p j) h d -> p j (h d)", j=TILES))
             k_b = loads.tile([P, PACK, H * DH], BF16, name="k_sb%d" % b)
-            nc.sync.dma_start(out=k_b[:], in_=k_rot[b].rearrange("(p t) h d -> p t (h d)", t=PACK))
+            nc.sync.dma_start(out=k_b[:], in_=k_rot[b].rearrange("(t p) h d -> p t (h d)", t=PACK))
             cv_sb.append(cv_b)
             q_sb.append(q_b)
             k_sb.append(k_b)
@@ -81,7 +80,7 @@ def tile_multiheadlatentattention_pb_t_kernel(tc, q_rot, k_rot, c_v, W_v_dec, ou
             in_=w_grouped[:].rearrange("p g n t -> p (g n t)"),
         )
 
-        score_ps, z_sb, neg_max, e_rows, eT_ps, eT_sb = {}, {}, {}, {}, {}, {}
+        score_ps, z_sb, neg_max, e_rows, eT_ps = {}, {}, {}, {}, {}
         row_sum, inv_sum, e_grouped, e_codes, e_scales, ctx_ps = {}, {}, {}, {}, {}, {}
         cvT_ps, cv_grouped, cv_codes, cv_scales = {}, {}, {}, {}
         v_ps, v_grouped, v_codes, v_scales = {}, {}, {}, {}
@@ -124,28 +123,20 @@ def tile_multiheadlatentattention_pb_t_kernel(tc, q_rot, k_rot, c_v, W_v_dec, ou
             e_rows[u] = e_tile
 
         def e_transposes(u):
-            eT_bank = eT_banks.tile([P, PACK, P], BF16)
-            for t in range(PACK):
-                nc.tensor.transpose(eT_bank[:, t, :], e_rows[u][:, t * P : (t + 1) * P], ident_bf[:])
+            words = e_rows[u][:].bitcast(F32)
+            eT_bank = eT_banks.tile([P, PACK, P], F32)
+            for half in range(2):
+                nc.tensor.transpose(eT_bank[:, half, :], words[:, half * P : (half + 1) * P], ident_f32[:])
             eT_ps[u] = eT_bank
 
         def copy_eT(u):
-            eT_tile = four.tile([P, PACK, P], BF16)
-            nc.scalar.copy(out=eT_tile[:], in_=eT_ps[u][:])
-            eT_sb[u] = eT_tile
-
-        def regroup_e(u):
             i, j = divmod(u, TILES)
             if j == 0:
-                e_group = three.tile([P, TILES, P, PACK], BF16, align_bytes=64)
+                e_group = three.tile([P, TILES, P * PACK], BF16, align_bytes=64)
                 e_grouped[i] = e_group
-            nc.gpsimd.tensor_scalar(
-                out=e_grouped[i][:, j],
-                in0=eT_sb[u][:].rearrange("p t q -> p q t"),
-                scalar1=1.0,
-                scalar2=0.0,
-                op0=MULT,
-                op1=ADD,
+            nc.scalar.copy(
+                out=e_grouped[i][:, j, :].bitcast(F32).rearrange("p (q u) -> p q u", u=2),
+                in_=eT_ps[u][:, 0:2, :].rearrange("p u q -> p q u"),
             )
 
         def latent_transposes(i):
@@ -234,7 +225,7 @@ def tile_multiheadlatentattention_pb_t_kernel(tc, q_rot, k_rot, c_v, W_v_dec, ou
             nc.vector.quantize_mx(
                 out=e_code[:].bitcast(FP8X4),
                 scales=e_scale[:],
-                in_=e_grouped[i][:].rearrange("p j q t -> p (j q t)"),
+                in_=e_grouped[i][:].rearrange("p j n -> p (j n)"),
             )
             e_codes[i], e_scales[i] = e_code, e_scale
 
@@ -287,7 +278,6 @@ def tile_multiheadlatentattention_pb_t_kernel(tc, q_rot, k_rot, c_v, W_v_dec, ou
             unit_step(scale_and_min, u + 2)
             unit_step(exponential, u + 1)
             unit_step(copy_eT, u - 1)
-            unit_step(regroup_e, u - 2)
 
         stack.enter_context(tc.manual_schedule())
         for r in range(-LATENT_LEAD, HEADS + STORE_LAG):

@@ -14,7 +14,9 @@ U8 = mybir.dt.uint8
 FP8X4 = mybir.dt.float8_e4m3fn_x4
 EXP = mybir.ActivationFunctionType.Exp
 MULT = mybir.AluOpType.mult
-MIN = mybir.AluOpType.min
+ADD = mybir.AluOpType.add
+MAX = mybir.AluOpType.max
+AXIS_X = mybir.AxisListType.X
 
 P = 128
 PACK = 4
@@ -80,7 +82,7 @@ def tile_multiheadlatentattention_pb_t_kernel(tc, q_rot, k_rot, c_v, W_v_dec, ou
             in_=w_grouped[:].rearrange("p g n t -> p (g n t)"),
         )
 
-        score_ps, z_sb, neg_max, e_rows, eT_ps = {}, {}, {}, {}, {}
+        score_ps, neg_max, e_rows, eT_ps = {}, {}, {}, {}
         row_sum, inv_sum, e_grouped, e_codes, e_scales, ctx_ps = {}, {}, {}, {}, {}, {}
         cvT_ps, cv_grouped, cv_codes, cv_scales = {}, {}, {}, {}
         v_ps, v_grouped, v_codes, v_scales = {}, {}, {}, {}
@@ -98,13 +100,14 @@ def tile_multiheadlatentattention_pb_t_kernel(tc, q_rot, k_rot, c_v, W_v_dec, ou
             )
             score_ps[u] = score_bank
 
-        def scale_and_min(u):
-            z = four.tile([P, S], F32)
-            z_min = six.tile([P, 1], F32)
-            nc.vector.tensor_scalar(
-                out=z[:], in0=score_ps[u][:], scalar1=-SCALE, scalar2=None, op0=MULT, op1=MIN, accum_out=z_min[:]
+        def row_max(u):
+            s_max = six.tile([P, 1], F32)
+            nc.vector.tensor_reduce(out=s_max[:], in_=score_ps[u][:], axis=AXIS_X, op=MAX)
+            bias = six.tile([P, 1], F32)
+            nc.gpsimd.tensor_scalar(
+                out=bias[:], in0=s_max[:], scalar1=-SCALE, scalar2=0.0, op0=MULT, op1=ADD
             )
-            z_sb[u], neg_max[u] = z, z_min
+            neg_max[u] = bias
 
         def exponential(u):
             i, j = divmod(u, TILES)
@@ -114,10 +117,10 @@ def tile_multiheadlatentattention_pb_t_kernel(tc, q_rot, k_rot, c_v, W_v_dec, ou
             e_tile = four.tile([P, S], BF16)
             nc.scalar.activation(
                 out=e_tile[:],
-                in_=z_sb[u][:],
+                in_=score_ps[u][:],
                 func=EXP,
                 bias=neg_max[u][:],
-                scale=-1.0,
+                scale=SCALE,
                 accum_out=row_sum[i][:, j : j + 1],
             )
             e_rows[u] = e_tile
@@ -275,7 +278,7 @@ def tile_multiheadlatentattention_pb_t_kernel(tc, q_rot, k_rot, c_v, W_v_dec, ou
         def beat(u):
             unit_step(scores, u + 3)
             unit_step(e_transposes, u)
-            unit_step(scale_and_min, u + 2)
+            unit_step(row_max, u + 2)
             unit_step(exponential, u + 1)
             unit_step(copy_eT, u - 1)
 

@@ -126,20 +126,22 @@ def tile_multiheadlatentattention_pb_t_kernel(tc, q_rot, k_rot, c_v, W_v_dec, ou
             e_rows[u] = e_tile
 
         def e_transposes(u):
+            if u % 2 == 0:
+                eT_pair = eT_banks.tile([P, 2, 2, P], F32)
+                eT_ps[u] = eT_ps[u + 1] = eT_pair
             words = e_rows[u][:].bitcast(F32)
-            eT_bank = eT_banks.tile([P, PACK, P], F32)
             for half in range(2):
-                nc.tensor.transpose(eT_bank[:, half, :], words[:, half * P : (half + 1) * P], ident_f32[:])
-            eT_ps[u] = eT_bank
+                nc.tensor.transpose(eT_ps[u][:, u % 2, half, :], words[:, half * P : (half + 1) * P], ident_f32[:])
 
-        def copy_eT(u):
+        def copy_eT_pair(u):
             i, j = divmod(u, TILES)
             if j == 0:
-                e_group = three.tile([P, TILES, P * PACK], BF16, align_bytes=64)
+                e_group = three.tile([P, TILES * P * PACK], BF16, align_bytes=64)
                 e_grouped[i] = e_group
+            pair_cols = slice(j * P * PACK, (j + 2) * P * PACK)
             nc.scalar.copy(
-                out=e_grouped[i][:, j, :].bitcast(F32).rearrange("p (q u) -> p q u", u=2),
-                in_=eT_ps[u][:, 0:2, :].rearrange("p u q -> p q u"),
+                out=e_grouped[i][:, pair_cols].bitcast(F32).rearrange("p (j q u) -> p j q u", j=2, u=2),
+                in_=eT_ps[u][:].rearrange("p j u q -> p j q u"),
             )
 
         def latent_transposes(i):
@@ -228,7 +230,7 @@ def tile_multiheadlatentattention_pb_t_kernel(tc, q_rot, k_rot, c_v, W_v_dec, ou
             nc.vector.quantize_mx(
                 out=e_code[:].bitcast(FP8X4),
                 scales=e_scale[:],
-                in_=e_grouped[i][:].rearrange("p j n -> p (j n)"),
+                in_=e_grouped[i][:],
             )
             e_codes[i], e_scales[i] = e_code, e_scale
 
@@ -280,7 +282,8 @@ def tile_multiheadlatentattention_pb_t_kernel(tc, q_rot, k_rot, c_v, W_v_dec, ou
             unit_step(e_transposes, u)
             unit_step(row_max, u + 2)
             unit_step(exponential, u + 1)
-            unit_step(copy_eT, u - 1)
+            if u % 2 == 0:
+                unit_step(copy_eT_pair, u - 2)
 
         stack.enter_context(tc.manual_schedule())
         for r in range(-LATENT_LEAD, HEADS + STORE_LAG):
@@ -289,17 +292,17 @@ def tile_multiheadlatentattention_pb_t_kernel(tc, q_rot, k_rot, c_v, W_v_dec, ou
             side_job(normalise_and_store, r - STORE_LAG)
 
             beat(TILES * r + 1)
-            side_job(qk_transposes, r + QK_LEAD)
             side_job(regroup_latent, r + LATENT_LEAD)
             side_job(regroup_values, r - QUANTISE_LAG)
             side_job(invert_sums, r - CONTEXT_LAG)
 
             beat(TILES * r + 2)
-            side_job(copy_qk, r + QK_LEAD)
+            side_job(qk_transposes, r + QK_LEAD)
             side_job(quantise_latent, r + LATENT_LEAD)
             side_job(quantise_e, r - QUANTISE_LAG)
 
             beat(TILES * r + 3)
+            side_job(copy_qk, r + QK_LEAD)
             side_job(context_passes, r - CONTEXT_LAG)
             side_job(value_passes, r)
             side_job(quantise_values, r - QUANTISE_LAG)

@@ -26,11 +26,19 @@ HEADS = B * H
 UNITS = HEADS * TILES
 SCALE = 1.0 / math.sqrt(DH)
 
-QK_LEAD = 2
-LATENT_LEAD = TILES
-QUANTISE_LAG = 1
-CONTEXT_LAG = 2
-STORE_LAG = 3
+def latent_beat(i):
+    return TILES * (i - 2) if i >= PACK else 2 * i
+
+
+def value_beat(i):
+    return min(TILES * i + 7, UNITS - 1) if i >= PACK else (11, 13, 15, 19)[i]
+
+
+def context_beat(i):
+    return min(TILES * i + 11, UNITS + 3) if i >= PACK - 1 else (15, 17, 19)[i]
+
+
+W_PIECES = 8
 
 assert TILES == PACK
 assert B * PACK == HEADS
@@ -45,23 +53,28 @@ def tile_multiheadlatentattention_pb_t_kernel(tc, q_rot, k_rot, c_v, W_v_dec, ou
         three = stack.enter_context(tc.tile_pool(name="three", bufs=3))
         four = stack.enter_context(tc.tile_pool(name="four", bufs=4))
         six = stack.enter_context(tc.tile_pool(name="six", bufs=6))
+        eight = stack.enter_context(tc.tile_pool(name="eight", bufs=8))
         score_banks = stack.enter_context(tc.psum_pool(name="score_banks", bufs=3))
         eT_banks = stack.enter_context(tc.psum_pool(name="eT_banks", bufs=2))
         side_banks = stack.enter_context(tc.psum_pool(name="side_banks", bufs=3))
 
-        w_raw = consts.tile([P, L_PASSES, PACK, H * DH], BF16)
-        nc.sync.dma_start(
-            out=w_raw[:].rearrange("p g (u e) n -> p (g u) (e n)", u=2, e=2),
-            in_=W_v_dec.rearrange("(a p e) n -> p a (e n)", p=P, e=2),
-        )
         cv_sb, q_sb, k_sb = [], [], []
         for b in range(B):
-            cv_b = loads.tile([P, PACK, DV], BF16, name="cv_sb%d" % b)
-            nc.sync.dma_start(out=cv_b[:].rearrange("p (u e) l -> p u (e l)", u=2), in_=c_v[b].rearrange("(u p e) l -> p u (e l)", u=2, e=2))
-            q_b = loads.tile([P, TILES, H * DH], BF16, name="q_sb%d" % b)
-            nc.sync.dma_start(out=q_b[:], in_=q_rot[b].rearrange("(p j) h d -> p j (h d)", j=TILES))
             k_b = loads.tile([P, PACK, H * DH], BF16, name="k_sb%d" % b)
             nc.sync.dma_start(out=k_b[:], in_=k_rot[b].rearrange("(t p) h d -> p t (h d)", t=PACK))
+            q_b = loads.tile([P, TILES, H * DH], BF16, name="q_sb%d" % b)
+            nc.sync.dma_start(out=q_b[:], in_=q_rot[b].rearrange("(p j) h d -> p j (h d)", j=TILES))
+            cv_b = loads.tile([P, PACK, DV], BF16, name="cv_sb%d" % b)
+            nc.sync.dma_start(
+                out=cv_b[:].rearrange("p (u e) l -> p u (e l)", u=2),
+                in_=c_v[b].rearrange("(u p e) l -> p u (e l)", u=2, e=2),
+            )
+            if b == 0:
+                w_raw = consts.tile([P, L_PASSES, PACK, H * DH], BF16, name="w_raw")
+                nc.sync.dma_start(
+                    out=w_raw[:].rearrange("p g (u e) n -> p (g u) (e n)", u=2, e=2),
+                    in_=W_v_dec.rearrange("(a p e) n -> p a (e n)", p=P, e=2),
+                )
             cv_sb.append(cv_b)
             q_sb.append(q_b)
             k_sb.append(k_b)
@@ -72,15 +85,27 @@ def tile_multiheadlatentattention_pb_t_kernel(tc, q_rot, k_rot, c_v, W_v_dec, ou
         make_identity(nc, ident_f32[:])
 
         w_grouped = consts.tile([P, L_PASSES, H * DH, PACK], BF16, align_bytes=64)
-        for g in range(L_PASSES):
-            nc.vector.tensor_copy(out=w_grouped[:, g], in_=w_raw[:, g].rearrange("p t n -> p n t"))
         w_codes = consts.tile([P, L_PASSES, H * DH], U32, align_bytes=64)
         w_scales = consts.tile([P, L_PASSES, H * DH], U8, align_bytes=64)
-        nc.vector.quantize_mx(
-            out=w_codes[:].rearrange("p g n -> p (g n)").bitcast(FP8X4),
-            scales=w_scales[:].rearrange("p g n -> p (g n)"),
-            in_=w_grouped[:].rearrange("p g n t -> p (g n t)"),
-        )
+
+        def regroup_weights(piece):
+            g, c = divmod(piece, W_PIECES)
+            cols = slice(c * (H * DH // W_PIECES), (c + 1) * (H * DH // W_PIECES))
+            nc.gpsimd.tensor_scalar(
+                out=w_grouped[:, g, cols],
+                in0=w_raw[:, g, :, cols].rearrange("p t n -> p n t"),
+                scalar1=1.0,
+                scalar2=0.0,
+                op0=MULT,
+                op1=ADD,
+            )
+
+        def quantise_weights(g):
+            nc.vector.quantize_mx(
+                out=w_codes[:, g].bitcast(FP8X4),
+                scales=w_scales[:, g],
+                in_=w_grouped[:, g].rearrange("p n t -> p (n t)"),
+            )
 
         score_ps, neg_max, e_rows, eT_ps = {}, {}, {}, {}
         row_sum, inv_sum, e_grouped, e_codes, e_scales, ctx_ps = {}, {}, {}, {}, {}, {}
@@ -112,7 +137,7 @@ def tile_multiheadlatentattention_pb_t_kernel(tc, q_rot, k_rot, c_v, W_v_dec, ou
         def exponential(u):
             i, j = divmod(u, TILES)
             if j == 0:
-                sums = six.tile([P, TILES], F32)
+                sums = eight.tile([P, TILES], F32)
                 row_sum[i] = sums
             e_tile = four.tile([P, S], BF16)
             nc.scalar.activation(
@@ -156,7 +181,8 @@ def tile_multiheadlatentattention_pb_t_kernel(tc, q_rot, k_rot, c_v, W_v_dec, ou
 
         def regroup_latent(i):
             cv_group = two.tile([P, L_PASSES * P * PACK], BF16, align_bytes=64)
-            nc.scalar.copy(
+            copy = nc.vector.tensor_copy if i < PACK else nc.scalar.copy
+            copy(
                 out=cv_group[:].bitcast(F32).rearrange("p (g s u) -> p g s u", g=L_PASSES, u=2),
                 in_=cvT_ps[i][:].rearrange("p g u s -> p g s u"),
             )
@@ -225,8 +251,8 @@ def tile_multiheadlatentattention_pb_t_kernel(tc, q_rot, k_rot, c_v, W_v_dec, ou
             qkT[i] = qkT_tile
 
         def quantise_e(i):
-            e_code = three.tile([P, S], U32, align_bytes=64)
-            e_scale = three.tile([P, S], U8, align_bytes=64)
+            e_code = six.tile([P, S], U32, align_bytes=64)
+            e_scale = six.tile([P, S], U8, align_bytes=64)
             nc.vector.quantize_mx(
                 out=e_code[:].bitcast(FP8X4),
                 scales=e_scale[:],
@@ -257,7 +283,7 @@ def tile_multiheadlatentattention_pb_t_kernel(tc, q_rot, k_rot, c_v, W_v_dec, ou
 
         def normalise_and_store(i):
             b, h = divmod(i, H)
-            result = three.tile([P, TILES, DH], F32)
+            result = six.tile([P, TILES, DH], F32)
             nc.vector.tensor_tensor(
                 out=result[:],
                 in0=ctx_ps[i][:],
@@ -269,40 +295,42 @@ def tile_multiheadlatentattention_pb_t_kernel(tc, q_rot, k_rot, c_v, W_v_dec, ou
                 in_=result[:],
             )
 
+        side_jobs = {}
+
+        def at(beat, job, i):
+            side_jobs.setdefault(beat, []).append((job, i))
+
+        for g in range(L_PASSES):
+            at(9 + g, quantise_weights, g)
+        for piece in range(L_PASSES * W_PIECES):
+            at(piece // 2, regroup_weights, piece)
+        for i in range(HEADS):
+            qk_beat = -1 if i == 1 else TILES * i - 6
+            at(context_beat(i) + 1, normalise_and_store, i)
+            at(value_beat(i) + 2, regroup_values, i)
+            at(qk_beat, qk_transposes, i)
+            at(qk_beat + 1, copy_qk, i)
+            at(latent_beat(i), latent_transposes, i)
+            at(latent_beat(i) + 1, regroup_latent, i)
+            at(context_beat(i) - 1, invert_sums, i)
+            at(latent_beat(i) + 2, quantise_latent, i)
+            at(value_beat(i) + 3, quantise_values, i)
+            at(TILES * i + 7, quantise_e, i)
+        for i in range(HEADS):
+            at(context_beat(i), context_passes, i)
+            at(value_beat(i), value_passes, i)
+
         def unit_step(step, u):
             if 0 <= u < UNITS:
                 step(u)
 
-        def side_job(job, i):
-            if 0 <= i < HEADS:
-                job(i)
-
-        def beat(u):
-            unit_step(scores, u + 3)
-            unit_step(e_transposes, u)
-            unit_step(row_max, u + 2)
-            unit_step(exponential, u + 1)
-            if u % 2 == 0:
-                unit_step(copy_eT_pair, u - 2)
-
         stack.enter_context(tc.manual_schedule())
-        for r in range(-LATENT_LEAD, HEADS + STORE_LAG):
-            beat(TILES * r)
-            side_job(latent_transposes, r + LATENT_LEAD)
-            side_job(normalise_and_store, r - STORE_LAG)
-
-            beat(TILES * r + 1)
-            side_job(regroup_latent, r + LATENT_LEAD)
-            side_job(regroup_values, r - QUANTISE_LAG)
-            side_job(invert_sums, r - CONTEXT_LAG)
-
-            beat(TILES * r + 2)
-            side_job(qk_transposes, r + QK_LEAD)
-            side_job(quantise_latent, r + LATENT_LEAD)
-            side_job(quantise_e, r - QUANTISE_LAG)
-
-            beat(TILES * r + 3)
-            side_job(copy_qk, r + QK_LEAD)
-            side_job(context_passes, r - CONTEXT_LAG)
-            side_job(value_passes, r)
-            side_job(quantise_values, r - QUANTISE_LAG)
+        for beat in range(min(side_jobs), max(side_jobs) + 1):
+            unit_step(scores, beat + 3)
+            unit_step(e_transposes, beat)
+            unit_step(row_max, beat + 2)
+            unit_step(exponential, beat + 1)
+            if beat % 2 == 0:
+                unit_step(copy_eT_pair, beat - 2)
+            for job, i in side_jobs.get(beat, []):
+                job(i)

@@ -14,6 +14,7 @@ U8 = mybir.dt.uint8
 FP8X4 = mybir.dt.float8_e4m3fn_x4
 EXP = mybir.ActivationFunctionType.Exp
 MULT = mybir.AluOpType.mult
+POW = mybir.AluOpType.pow
 ADD = mybir.AluOpType.add
 MAX = mybir.AluOpType.max
 AXIS_X = mybir.AxisListType.X
@@ -31,14 +32,17 @@ def latent_beat(i):
 
 
 def value_beat(i):
-    return min(TILES * i + 7, UNITS - 1) if i >= PACK else (11, 13, 15, 19)[i]
+    if i < PACK:
+        return (11, 13, 15, 19)[i]
+    return 2 * i + 63 if i >= HEADS - PACK else TILES * i + 7
 
 
 def context_beat(i):
-    return min(TILES * i + 11, UNITS + 3) if i >= PACK - 1 else (15, 17, 19)[i]
+    return min(TILES * i + 11, UNITS) if i >= PACK - 1 else (15, 17, 19)[i]
 
 
 W_PIECES = 8
+S_VALUES = HEADS - 3
 
 assert TILES == PACK
 assert B * PACK == HEADS
@@ -61,9 +65,15 @@ def tile_multiheadlatentattention_pb_t_kernel(tc, q_rot, k_rot, c_v, W_v_dec, ou
         cv_sb, q_sb, k_sb = [], [], []
         for b in range(B):
             k_b = loads.tile([P, PACK, H * DH], BF16, name="k_sb%d" % b)
-            nc.sync.dma_start(out=k_b[:], in_=k_rot[b].rearrange("(t p) h d -> p t (h d)", t=PACK))
             q_b = loads.tile([P, TILES, H * DH], BF16, name="q_sb%d" % b)
-            nc.sync.dma_start(out=q_b[:], in_=q_rot[b].rearrange("(p j) h d -> p j (h d)", j=TILES))
+            for heads in [slice(0, 1), slice(1, H)] if b == 0 else [slice(0, H)]:
+                cols = slice(heads.start * DH, heads.stop * DH)
+                nc.sync.dma_start(
+                    out=k_b[:, :, cols], in_=k_rot[b, :, heads].rearrange("(t p) h d -> p t (h d)", t=PACK)
+                )
+                nc.sync.dma_start(
+                    out=q_b[:, :, cols], in_=q_rot[b, :, heads].rearrange("(p j) h d -> p j (h d)", j=TILES)
+                )
             cv_b = loads.tile([P, PACK, DV], BF16, name="cv_sb%d" % b)
             nc.sync.dma_start(
                 out=cv_b[:].rearrange("p (u e) l -> p u (e l)", u=2),
@@ -106,6 +116,9 @@ def tile_multiheadlatentattention_pb_t_kernel(tc, q_rot, k_rot, c_v, W_v_dec, ou
                 scales=w_scales[:, g],
                 in_=w_grouped[:, g].rearrange("p n t -> p (n t)"),
             )
+
+        minus_one = consts.tile([P, TILES], F32)
+        nc.gpsimd.memset(minus_one[:], -1.0)
 
         score_ps, neg_max, e_rows, eT_ps = {}, {}, {}, {}
         row_sum, inv_sum, e_grouped, e_codes, e_scales, ctx_ps = {}, {}, {}, {}, {}, {}
@@ -220,7 +233,8 @@ def tile_multiheadlatentattention_pb_t_kernel(tc, q_rot, k_rot, c_v, W_v_dec, ou
 
         def regroup_values(i):
             v_group = two.tile([P, DH, PACK], BF16, align_bytes=64)
-            nc.vector.tensor_copy(out=v_group[:], in_=v_ps[i][:].rearrange("p t d -> p d t"))
+            copy = nc.scalar.copy if i >= S_VALUES else nc.vector.tensor_copy
+            copy(out=v_group[:], in_=v_ps[i][:].rearrange("p t d -> p d t"))
             v_grouped[i] = v_group
 
         def quantise_values(i):
@@ -250,25 +264,27 @@ def tile_multiheadlatentattention_pb_t_kernel(tc, q_rot, k_rot, c_v, W_v_dec, ou
             nc.scalar.copy(out=qkT_tile[:], in_=qkT_ps[i][:].rearrange("p a j s -> p a (j s)"))
             qkT[i] = qkT_tile
 
-        def quantise_e(i):
-            e_code = six.tile([P, S], U32, align_bytes=64)
-            e_scale = six.tile([P, S], U8, align_bytes=64)
+        def quantise_e(i, first=0, last=TILES):
+            if first == 0:
+                e_code = six.tile([P, S], U32, align_bytes=64)
+                e_scale = six.tile([P, S], U8, align_bytes=64)
+                e_codes[i], e_scales[i] = e_code, e_scale
+            cols = slice(first * P, last * P)
             nc.vector.quantize_mx(
-                out=e_code[:].bitcast(FP8X4),
-                scales=e_scale[:],
-                in_=e_grouped[i][:],
+                out=e_codes[i][:, cols].bitcast(FP8X4),
+                scales=e_scales[i][:, cols],
+                in_=e_grouped[i][:, first * P * PACK : last * P * PACK],
             )
-            e_codes[i], e_scales[i] = e_code, e_scale
 
         def invert_sums(i):
             inverse = three.tile([P, TILES], F32)
-            nc.vector.reciprocal(out=inverse[:], in_=row_sum[i][:])
+            nc.gpsimd.tensor_tensor(out=inverse[:], in0=row_sum[i][:], in1=minus_one[:], op=POW)
             inv_sum[i] = inverse
 
-        def context_passes(i):
+        def context_passes(i, first=0, last=TILES):
             b, h = divmod(i, H)
             ctx_bank = side_banks.tile([P, TILES, DH], F32, tag="side")
-            for j in range(TILES):
+            for j in range(first, last):
                 query_cols = slice(j * P, (j + 1) * P)
                 nc.tensor.matmul_mx(
                     out=ctx_bank[:, j, :],
@@ -281,32 +297,34 @@ def tile_multiheadlatentattention_pb_t_kernel(tc, q_rot, k_rot, c_v, W_v_dec, ou
                 )
             ctx_ps[i] = ctx_bank
 
-        def normalise_and_store(i):
+        def normalise_and_store(i, first=0, last=TILES):
             b, h = divmod(i, H)
             result = six.tile([P, TILES, DH], F32)
             nc.vector.tensor_tensor(
-                out=result[:],
-                in0=ctx_ps[i][:],
-                in1=inv_sum[i][:].unsqueeze(2).to_broadcast([P, TILES, DH]),
+                out=result[:, first:last],
+                in0=ctx_ps[i][:, first:last],
+                in1=inv_sum[i][:, first:last].unsqueeze(2).to_broadcast([P, last - first, DH]),
                 op=MULT,
             )
             nc.sync.dma_start(
-                out=out[b].rearrange("(p j) n -> p j n", j=TILES)[:, :, h * DH : (h + 1) * DH],
-                in_=result[:],
+                out=out[b].rearrange("(p j) n -> p j n", j=TILES)[:, first:last, h * DH : (h + 1) * DH],
+                in_=result[:, first:last],
             )
 
         side_jobs = {}
 
-        def at(beat, job, i):
-            side_jobs.setdefault(beat, []).append((job, i))
+        def at(beat, job, *args):
+            side_jobs.setdefault(beat, []).append((job, args))
 
+        LAST = HEADS - 1
         for g in range(L_PASSES):
             at(9 + g, quantise_weights, g)
         for piece in range(L_PASSES * W_PIECES):
             at(piece // 2, regroup_weights, piece)
         for i in range(HEADS):
             qk_beat = -1 if i == 1 else TILES * i - 6
-            at(context_beat(i) + 1, normalise_and_store, i)
+            if i < LAST:
+                at(context_beat(i) + 1, normalise_and_store, i)
             at(value_beat(i) + 2, regroup_values, i)
             at(qk_beat, qk_transposes, i)
             at(qk_beat + 1, copy_qk, i)
@@ -315,10 +333,17 @@ def tile_multiheadlatentattention_pb_t_kernel(tc, q_rot, k_rot, c_v, W_v_dec, ou
             at(context_beat(i) - 1, invert_sums, i)
             at(latent_beat(i) + 2, quantise_latent, i)
             at(value_beat(i) + 3, quantise_values, i)
-            at(TILES * i + 7, quantise_e, i)
-        for i in range(HEADS):
+            if i < LAST:
+                at(TILES * i + 7, quantise_e, i)
+        at(UNITS, quantise_e, LAST, 0, 2)
+        at(UNITS + 2, quantise_e, LAST, 2, TILES)
+        for i in range(LAST):
             at(context_beat(i), context_passes, i)
             at(value_beat(i), value_passes, i)
+        at(value_beat(LAST), value_passes, LAST)
+        for half in range(2):
+            at(UNITS + 2 + half, context_passes, LAST, 2 * half, 2 * half + 2)
+            at(UNITS + 2 + half, normalise_and_store, LAST, 2 * half, 2 * half + 2)
 
         def unit_step(step, u):
             if 0 <= u < UNITS:
@@ -332,5 +357,5 @@ def tile_multiheadlatentattention_pb_t_kernel(tc, q_rot, k_rot, c_v, W_v_dec, ou
             unit_step(exponential, beat + 1)
             if beat % 2 == 0:
                 unit_step(copy_eT_pair, beat - 2)
-            for job, i in side_jobs.get(beat, []):
-                job(i)
+            for job, args in side_jobs.get(beat, []):
+                job(*args)

@@ -14,7 +14,6 @@ U8 = mybir.dt.uint8
 FP8X4 = mybir.dt.float8_e4m3fn_x4
 EXP = mybir.ActivationFunctionType.Exp
 MULT = mybir.AluOpType.mult
-POW = mybir.AluOpType.pow
 ADD = mybir.AluOpType.add
 MAX = mybir.AluOpType.max
 AXIS_X = mybir.AxisListType.X
@@ -116,9 +115,6 @@ def tile_multiheadlatentattention_pb_t_kernel(tc, q_rot, k_rot, c_v, W_v_dec, ou
                 scales=w_scales[:, g],
                 in_=w_grouped[:, g].rearrange("p n t -> p (n t)"),
             )
-
-        minus_one = consts.tile([P, TILES], F32)
-        nc.gpsimd.memset(minus_one[:], -1.0)
 
         score_ps, neg_max, e_rows, eT_ps = {}, {}, {}, {}
         row_sum, inv_sum, e_grouped, e_codes, e_scales, ctx_ps = {}, {}, {}, {}, {}, {}
@@ -278,7 +274,7 @@ def tile_multiheadlatentattention_pb_t_kernel(tc, q_rot, k_rot, c_v, W_v_dec, ou
 
         def invert_sums(i):
             inverse = three.tile([P, TILES], F32)
-            nc.gpsimd.tensor_tensor(out=inverse[:], in0=row_sum[i][:], in1=minus_one[:], op=POW)
+            nc.vector.reciprocal(out=inverse[:], in_=row_sum[i][:])
             inv_sum[i] = inverse
 
         def context_passes(i, first=0, last=TILES):

@@ -54,11 +54,11 @@ def tile_multiheadlatentattention_pb_t_kernel(tc, q_rot, k_rot, c_v, W_v_dec, ou
         consts = stack.enter_context(tc.tile_pool(name="consts", bufs=1))
         two = stack.enter_context(tc.tile_pool(name="two", bufs=2))
         three = stack.enter_context(tc.tile_pool(name="three", bufs=3))
-        four = stack.enter_context(tc.tile_pool(name="four", bufs=4))
+        five = stack.enter_context(tc.tile_pool(name="five", bufs=5))
         six = stack.enter_context(tc.tile_pool(name="six", bufs=6))
         eight = stack.enter_context(tc.tile_pool(name="eight", bufs=8))
-        score_banks = stack.enter_context(tc.psum_pool(name="score_banks", bufs=3))
-        eT_banks = stack.enter_context(tc.psum_pool(name="eT_banks", bufs=2))
+        score_banks = stack.enter_context(tc.psum_pool(name="score_banks", bufs=4))
+        eT_banks = stack.enter_context(tc.psum_pool(name="eT_banks", bufs=1))
         side_banks = stack.enter_context(tc.psum_pool(name="side_banks", bufs=3))
 
         cv_sb, q_sb, k_sb = [], [], []
@@ -148,7 +148,7 @@ def tile_multiheadlatentattention_pb_t_kernel(tc, q_rot, k_rot, c_v, W_v_dec, ou
             if j == 0:
                 sums = eight.tile([P, TILES], F32)
                 row_sum[i] = sums
-            e_tile = four.tile([P, S], BF16)
+            e_tile = five.tile([P, S], BF16)
             nc.scalar.activation(
                 out=e_tile[:],
                 in_=score_ps[u][:],
@@ -256,7 +256,7 @@ def tile_multiheadlatentattention_pb_t_kernel(tc, q_rot, k_rot, c_v, W_v_dec, ou
             qkT_ps[i] = qkT_bank
 
         def copy_qk(i):
-            qkT_tile = four.tile([P, 2, S], BF16)
+            qkT_tile = five.tile([P, 2, S], BF16)
             nc.scalar.copy(out=qkT_tile[:], in_=qkT_ps[i][:].rearrange("p a j s -> p a (j s)"))
             qkT[i] = qkT_tile
 
@@ -318,7 +318,7 @@ def tile_multiheadlatentattention_pb_t_kernel(tc, q_rot, k_rot, c_v, W_v_dec, ou
         for piece in range(L_PASSES * W_PIECES):
             at(piece // 2, regroup_weights, piece)
         for i in range(HEADS):
-            qk_beat = -1 if i == 1 else TILES * i - 6
+            qk_beat = -2 if i == 1 else TILES * i - 6
             if i < LAST:
                 at(context_beat(i) + 1, normalise_and_store, i)
             at(value_beat(i) + 2, regroup_values, i)
@@ -347,9 +347,11 @@ def tile_multiheadlatentattention_pb_t_kernel(tc, q_rot, k_rot, c_v, W_v_dec, ou
 
         stack.enter_context(tc.manual_schedule())
         for beat in range(min(side_jobs), max(side_jobs) + 1):
-            unit_step(scores, beat + 3)
-            unit_step(e_transposes, beat)
-            unit_step(row_max, beat + 2)
+            unit_step(scores, beat + 4)
+            if beat % 2 == 1:
+                unit_step(e_transposes, beat - 1)
+                unit_step(e_transposes, beat)
+            unit_step(row_max, beat + 3)
             unit_step(exponential, beat + 1)
             if beat % 2 == 0:
                 unit_step(copy_eT_pair, beat - 2)

@@ -37,7 +37,7 @@ def value_beat(i):
 
 
 def context_beat(i):
-    return min(TILES * i + 11, UNITS) if i >= PACK - 1 else (15, 17, 19)[i]
+    return min(TILES * i + 14, UNITS) if i >= PACK - 1 else (18, 20, 22)[i]
 
 
 W_PIECES = 8
@@ -145,9 +145,9 @@ def tile_multiheadlatentattention_pb_t_kernel(tc, q_rot, k_rot, c_v, W_v_dec, ou
 
         def exponential(u):
             i, j = divmod(u, TILES)
-            if j == 0:
-                sums = eight.tile([P, TILES], F32)
-                row_sum[i] = sums
+            if j == 0 and i % 2 == 0:
+                sums = eight.tile([P, 2, TILES], F32)
+                row_sum[i] = row_sum[i + 1] = sums
             e_tile = five.tile([P, S], BF16)
             nc.scalar.activation(
                 out=e_tile[:],
@@ -155,7 +155,7 @@ def tile_multiheadlatentattention_pb_t_kernel(tc, q_rot, k_rot, c_v, W_v_dec, ou
                 func=EXP,
                 bias=neg_max[u][:],
                 scale=SCALE,
-                accum_out=row_sum[i][:, j : j + 1],
+                accum_out=row_sum[i][:, i % 2, j : j + 1],
             )
             e_rows[u] = e_tile
 
@@ -257,7 +257,10 @@ def tile_multiheadlatentattention_pb_t_kernel(tc, q_rot, k_rot, c_v, W_v_dec, ou
 
         def copy_qk(i):
             qkT_tile = five.tile([P, 2, S], BF16)
-            nc.scalar.copy(out=qkT_tile[:], in_=qkT_ps[i][:].rearrange("p a j s -> p a (j s)"))
+            nc.scalar.copy(
+                out=qkT_tile[:].rearrange("p a s -> p (a s)").bitcast(F32),
+                in_=qkT_ps[i][:].rearrange("p a j s -> p (a j s)").bitcast(F32),
+            )
             qkT[i] = qkT_tile
 
         def quantise_e(i, first=0, last=TILES):
@@ -273,9 +276,9 @@ def tile_multiheadlatentattention_pb_t_kernel(tc, q_rot, k_rot, c_v, W_v_dec, ou
             )
 
         def invert_sums(i):
-            inverse = three.tile([P, TILES], F32)
+            inverse = three.tile([P, 2, TILES], F32)
             nc.vector.reciprocal(out=inverse[:], in_=row_sum[i][:])
-            inv_sum[i] = inverse
+            inv_sum[i] = inv_sum[i + 1] = inverse
 
         def context_passes(i, first=0, last=TILES):
             b, h = divmod(i, H)
@@ -299,7 +302,7 @@ def tile_multiheadlatentattention_pb_t_kernel(tc, q_rot, k_rot, c_v, W_v_dec, ou
             nc.vector.tensor_tensor(
                 out=result[:, first:last],
                 in0=ctx_ps[i][:, first:last],
-                in1=inv_sum[i][:, first:last].unsqueeze(2).to_broadcast([P, last - first, DH]),
+                in1=inv_sum[i][:, i % 2, first:last].unsqueeze(2).to_broadcast([P, last - first, DH]),
                 op=MULT,
             )
             nc.sync.dma_start(
@@ -321,12 +324,13 @@ def tile_multiheadlatentattention_pb_t_kernel(tc, q_rot, k_rot, c_v, W_v_dec, ou
             qk_beat = -2 if i == 1 else TILES * i - 6
             if i < LAST:
                 at(context_beat(i) + 1, normalise_and_store, i)
-            at(value_beat(i) + 2, regroup_values, i)
+            at(value_beat(i) + 1, regroup_values, i)
             at(qk_beat, qk_transposes, i)
             at(qk_beat + 1, copy_qk, i)
             at(latent_beat(i), latent_transposes, i)
             at(latent_beat(i) + 1, regroup_latent, i)
-            at(context_beat(i) - 1, invert_sums, i)
+            if i % 2 == 0:
+                at(context_beat(i) - 1, invert_sums, i)
             at(latent_beat(i) + 2, quantise_latent, i)
             at(value_beat(i) + 3, quantise_values, i)
             if i < LAST:

from contextlib import ExitStack
import math

import concourse.mybir as mybir
from concourse.masks import make_identity

B, S, H, DH, DV = 8, 512, 4, 128, 1024
FLOPS = 2 * B * S * DV * H * DH + 2 * 2 * B * H * S * S * DH

BF16 = mybir.dt.bfloat16
F32 = mybir.dt.float32
U32 = mybir.dt.uint32
U8 = mybir.dt.uint8
FP8X4 = mybir.dt.float8_e4m3fn_x4
EXP = mybir.ActivationFunctionType.Exp
MULT = mybir.AluOpType.mult
ADD = mybir.AluOpType.add
MAX = mybir.AluOpType.max
AXIS_X = mybir.AxisListType.X

P = 128
PACK = 4
TILES = S // P
L_PASSES = DV // (P * PACK)
HEADS = B * H
UNITS = HEADS * TILES
SCALE = 1.0 / math.sqrt(DH)

def latent_beat(i):
    return TILES * (i - 2) if i >= PACK else 2 * i


def value_beat(i):
    if i < PACK:
        return (11, 13, 15, 19)[i]
    return 2 * i + 63 if i >= HEADS - PACK else TILES * i + 7


def context_beat(i):
    return min(TILES * i + 14, UNITS) if i >= PACK - 1 else (18, 20, 22)[i]


W_PIECES = 8
S_VALUES = HEADS - 3

assert TILES == PACK
assert B * PACK == HEADS


def tile_multiheadlatentattention_pb_t_kernel(tc, q_rot, k_rot, c_v, W_v_dec, out):
    nc = tc.nc
    with ExitStack() as stack:
        loads = stack.enter_context(tc.tile_pool(name="loads", bufs=1))
        consts = stack.enter_context(tc.tile_pool(name="consts", bufs=1))
        two = stack.enter_context(tc.tile_pool(name="two", bufs=2))
        three = stack.enter_context(tc.tile_pool(name="three", bufs=3))
        five = stack.enter_context(tc.tile_pool(name="five", bufs=5))
        six = stack.enter_context(tc.tile_pool(name="six", bufs=6))
        eight = stack.enter_context(tc.tile_pool(name="eight", bufs=8))
        score_banks = stack.enter_context(tc.psum_pool(name="score_banks", bufs=4))
        eT_banks = stack.enter_context(tc.psum_pool(name="eT_banks", bufs=1))
        side_banks = stack.enter_context(tc.psum_pool(name="side_banks", bufs=3))

        cv_sb, q_sb, k_sb = [], [], []
        for b in range(B):
            k_b = loads.tile([P, PACK, H * DH], BF16, name="k_sb%d" % b)
            q_b = loads.tile([P, TILES, H * DH], BF16, name="q_sb%d" % b)
            for heads in [slice(0, 1), slice(1, H)] if b == 0 else [slice(0, H)]:
                cols = slice(heads.start * DH, heads.stop * DH)
                nc.sync.dma_start(
                    out=k_b[:, :, cols], in_=k_rot[b, :, heads].rearrange("(t p) h d -> p t (h d)", t=PACK)
                )
                nc.sync.dma_start(
                    out=q_b[:, :, cols], in_=q_rot[b, :, heads].rearrange("(p j) h d -> p j (h d)", j=TILES)
                )
            cv_b = loads.tile([P, PACK, DV], BF16, name="cv_sb%d" % b)
            nc.sync.dma_start(
                out=cv_b[:].rearrange("p (u e) l -> p u (e l)", u=2),
                in_=c_v[b].rearrange("(u p e) l -> p u (e l)", u=2, e=2),
            )
            if b == 0:
                w_raw = consts.tile([P, L_PASSES, PACK, H * DH], BF16, name="w_raw")
                nc.sync.dma_start(
                    out=w_raw[:].rearrange("p g (u e) n -> p (g u) (e n)", u=2, e=2),
                    in_=W_v_dec.rearrange("(a p e) n -> p a (e n)", p=P, e=2),
                )
            cv_sb.append(cv_b)
            q_sb.append(q_b)
            k_sb.append(k_b)

        ident_bf = consts.tile([P, P], BF16)
        make_identity(nc, ident_bf[:])
        ident_f32 = consts.tile([P, P], F32)
        make_identity(nc, ident_f32[:])

        w_grouped = consts.tile([P, L_PASSES, H * DH, PACK], BF16, align_bytes=64)
        w_codes = consts.tile([P, L_PASSES, H * DH], U32, align_bytes=64)
        w_scales = consts.tile([P, L_PASSES, H * DH], U8, align_bytes=64)

        def regroup_weights(piece):
            g, c = divmod(piece, W_PIECES)
            cols = slice(c * (H * DH // W_PIECES), (c + 1) * (H * DH // W_PIECES))
            nc.gpsimd.tensor_scalar(
                out=w_grouped[:, g, cols],
                in0=w_raw[:, g, :, cols].rearrange("p t n -> p n t"),
                scalar1=1.0,
                scalar2=0.0,
                op0=MULT,
                op1=ADD,
            )

        def quantise_weights(g):
            nc.vector.quantize_mx(
                out=w_codes[:, g].bitcast(FP8X4),
                scales=w_scales[:, g],
                in_=w_grouped[:, g].rearrange("p n t -> p (n t)"),
            )

        score_ps, neg_max, e_rows, eT_ps = {}, {}, {}, {}
        row_sum, inv_sum, e_grouped, e_codes, e_scales, ctx_ps = {}, {}, {}, {}, {}, {}
        cvT_ps, cv_grouped, cv_codes, cv_scales = {}, {}, {}, {}
        v_ps, v_grouped, v_codes, v_scales = {}, {}, {}, {}
        qkT_ps, qkT = {}, {}

        def scores(u):
            i, j = divmod(u, TILES)
            score_bank = score_banks.tile([P, S], F32)
            nc.tensor.matmul(
                score_bank[:],
                lhsT=qkT[i][:, 0, j * P : (j + 1) * P],
                rhs=qkT[i][:, 1, :],
                start=True,
                stop=True,
            )
            score_ps[u] = score_bank

        def row_max(u):
            s_max = six.tile([P, 1], F32)
            nc.vector.tensor_reduce(out=s_max[:], in_=score_ps[u][:], axis=AXIS_X, op=MAX)
            bias = six.tile([P, 1], F32)
            nc.gpsimd.tensor_scalar(
                out=bias[:], in0=s_max[:], scalar1=-SCALE, scalar2=0.0, op0=MULT, op1=ADD
            )
            neg_max[u] = bias

        def exponential(u):
            i, j = divmod(u, TILES)
            if j == 0 and i % 2 == 0:
                sums = eight.tile([P, 2, TILES], F32)
                row_sum[i] = row_sum[i + 1] = sums
            e_tile = five.tile([P, S], BF16)
            nc.scalar.activation(
                out=e_tile[:],
                in_=score_ps[u][:],
                func=EXP,
                bias=neg_max[u][:],
                scale=SCALE,
                accum_out=row_sum[i][:, i % 2, j : j + 1],
            )
            e_rows[u] = e_tile

        def e_transposes(u):
            if u % 2 == 0:
                eT_pair = eT_banks.tile([P, 2, 2, P], F32)
                eT_ps[u] = eT_ps[u + 1] = eT_pair
            words = e_rows[u][:].bitcast(F32)
            for half in range(2):
                nc.tensor.transpose(eT_ps[u][:, u % 2, half, :], words[:, half * P : (half + 1) * P], ident_f32[:])

        def copy_eT_pair(u):
            i, j = divmod(u, TILES)
            if j == 0:
                e_group = three.tile([P, TILES * P * PACK], BF16, align_bytes=64)
                e_grouped[i] = e_group
            pair_cols = slice(j * P * PACK, (j + 2) * P * PACK)
            nc.scalar.copy(
                out=e_grouped[i][:, pair_cols].bitcast(F32).rearrange("p (j q u) -> p j q u", j=2, u=2),
                in_=eT_ps[u][:].rearrange("p j u q -> p j q u"),
            )

        def latent_transposes(i):
            b, t = divmod(i, PACK)
            words = cv_sb[b][:, t, :].bitcast(F32)
            cvT_bank = side_banks.tile([P, L_PASSES, 2, P], F32, tag="side")
            for g in range(L_PASSES):
                for u in range(2):
                    first = (2 * g + u) * P
                    nc.tensor.transpose(cvT_bank[:, g, u, :], words[:, first : first + P], ident_f32[:])
            cvT_ps[i] = cvT_bank

        def regroup_latent(i):
            cv_group = two.tile([P, L_PASSES * P * PACK], BF16, align_bytes=64)
            copy = nc.vector.tensor_copy if i < PACK else nc.scalar.copy
            copy(
                out=cv_group[:].bitcast(F32).rearrange("p (g s u) -> p g s u", g=L_PASSES, u=2),
                in_=cvT_ps[i][:].rearrange("p g u s -> p g s u"),
            )
            cv_grouped[i] = cv_group

        def quantise_latent(i):
            b, t = divmod(i, PACK)
            if t == 0:
                cv_code = two.tile([P, PACK, L_PASSES * P], U32, align_bytes=64)
                cv_scale = two.tile([P, PACK, L_PASSES * P], U8, align_bytes=64)
                cv_codes[b], cv_scales[b] = cv_code, cv_scale
            nc.vector.quantize_mx(
                out=cv_codes[b][:, t, :].bitcast(FP8X4),
                scales=cv_scales[b][:, t, :],
                in_=cv_grouped[i][:],
            )

        def value_passes(i):
            b, h = divmod(i, H)
            head_cols = slice(h * DH, (h + 1) * DH)
            v_bank = side_banks.tile([P, PACK, DH], F32, tag="side")
            for t in range(PACK):
                for g in range(L_PASSES):
                    key_cols = slice(g * P, (g + 1) * P)
                    nc.tensor.matmul_mx(
                        out=v_bank[:, t, :],
                        lhsT=cv_codes[b][:, t, key_cols].bitcast(FP8X4),
                        lhsT_scale=cv_scales[b][:, t, key_cols],
                        rhs=w_codes[:, g, head_cols].bitcast(FP8X4),
                        rhs_scale=w_scales[:, g, head_cols],
                        start=(g == 0),
                        stop=(g == L_PASSES - 1),
                    )
            v_ps[i] = v_bank

        def regroup_values(i):
            v_group = two.tile([P, DH, PACK], BF16, align_bytes=64)
            copy = nc.scalar.copy if i >= S_VALUES else nc.vector.tensor_copy
            copy(out=v_group[:], in_=v_ps[i][:].rearrange("p t d -> p d t"))
            v_grouped[i] = v_group

        def quantise_values(i):
            b, h = divmod(i, H)
            if h == 0:
                v_code = two.tile([P, H, DH], U32, align_bytes=64)
                v_scale = two.tile([P, H, DH], U8, align_bytes=64)
                v_codes[b], v_scales[b] = v_code, v_scale
            nc.vector.quantize_mx(
                out=v_codes[b][:, h, :].bitcast(FP8X4),
                scales=v_scales[b][:, h, :],
                in_=v_grouped[i][:].rearrange("p d t -> p (d t)"),
            )

        def qk_transposes(i):
            b, h = divmod(i, H)
            head_cols = slice(h * DH, (h + 1) * DH)
            qkT_bank = side_banks.tile([P, 2, TILES, P], BF16, tag="side")
            for j in range(TILES):
                nc.tensor.transpose(qkT_bank[:, 0, j, :], q_sb[b][:, j, head_cols], ident_bf[:])
            for t in range(PACK):
                nc.tensor.transpose(qkT_bank[:, 1, t, :], k_sb[b][:, t, head_cols], ident_bf[:])
            qkT_ps[i] = qkT_bank

        def copy_qk(i):
            qkT_tile = five.tile([P, 2, S], BF16)
            nc.scalar.copy(
                out=qkT_tile[:].rearrange("p a s -> p (a s)").bitcast(F32),
                in_=qkT_ps[i][:].rearrange("p a j s -> p (a j s)").bitcast(F32),
            )
            qkT[i] = qkT_tile

        def quantise_e(i, first=0, last=TILES):
            if first == 0:
                e_code = six.tile([P, S], U32, align_bytes=64)
                e_scale = six.tile([P, S], U8, align_bytes=64)
                e_codes[i], e_scales[i] = e_code, e_scale
            cols = slice(first * P, last * P)
            nc.vector.quantize_mx(
                out=e_codes[i][:, cols].bitcast(FP8X4),
                scales=e_scales[i][:, cols],
                in_=e_grouped[i][:, first * P * PACK : last * P * PACK],
            )

        def invert_sums(i):
            inverse = three.tile([P, 2, TILES], F32)
            nc.vector.reciprocal(out=inverse[:], in_=row_sum[i][:])
            inv_sum[i] = inv_sum[i + 1] = inverse

        def context_passes(i, first=0, last=TILES):
            b, h = divmod(i, H)
            ctx_bank = side_banks.tile([P, TILES, DH], F32, tag="side")
            for j in range(first, last):
                query_cols = slice(j * P, (j + 1) * P)
                nc.tensor.matmul_mx(
                    out=ctx_bank[:, j, :],
                    lhsT=e_codes[i][:, query_cols].bitcast(FP8X4),
                    lhsT_scale=e_scales[i][:, query_cols],
                    rhs=v_codes[b][:, h, :].bitcast(FP8X4),
                    rhs_scale=v_scales[b][:, h, :],
                    start=True,
                    stop=True,
                )
            ctx_ps[i] = ctx_bank

        def normalise_and_store(i, first=0, last=TILES):
            b, h = divmod(i, H)
            result = six.tile([P, TILES, DH], F32)
            nc.vector.tensor_tensor(
                out=result[:, first:last],
                in0=ctx_ps[i][:, first:last],
                in1=inv_sum[i][:, i % 2, first:last].unsqueeze(2).to_broadcast([P, last - first, DH]),
                op=MULT,
            )
            nc.sync.dma_start(
                out=out[b].rearrange("(p j) n -> p j n", j=TILES)[:, first:last, h * DH : (h + 1) * DH],
                in_=result[:, first:last],
            )

        side_jobs = {}

        def at(beat, job, *args):
            side_jobs.setdefault(beat, []).append((job, args))

        LAST = HEADS - 1
        for g in range(L_PASSES):
            at(9 + g, quantise_weights, g)
        for piece in range(L_PASSES * W_PIECES):
            at(piece // 2, regroup_weights, piece)
        for i in range(HEADS):
            qk_beat = -2 if i == 1 else TILES * i - 6
            if i < LAST:
                at(context_beat(i) + 1, normalise_and_store, i)
            at(value_beat(i) + 1, regroup_values, i)
            at(qk_beat, qk_transposes, i)
            at(qk_beat + 1, copy_qk, i)
            at(latent_beat(i), latent_transposes, i)
            at(latent_beat(i) + 1, regroup_latent, i)
            if i % 2 == 0:
                at(context_beat(i) - 1, invert_sums, i)
            at(latent_beat(i) + 2, quantise_latent, i)
            at(value_beat(i) + 3, quantise_values, i)
            if i < LAST:
                at(TILES * i + 7, quantise_e, i)
        at(UNITS, quantise_e, LAST, 0, 2)
        at(UNITS + 2, quantise_e, LAST, 2, TILES)
        for i in range(LAST):
            at(context_beat(i), context_passes, i)
            at(value_beat(i), value_passes, i)
        at(value_beat(LAST), value_passes, LAST)
        for half in range(2):
            at(UNITS + 2 + half, context_passes, LAST, 2 * half, 2 * half + 2)
            at(UNITS + 2 + half, normalise_and_store, LAST, 2 * half, 2 * half + 2)

        def unit_step(step, u):
            if 0 <= u < UNITS:
                step(u)

        stack.enter_context(tc.manual_schedule())
        for beat in range(min(side_jobs), max(side_jobs) + 1):
            unit_step(scores, beat + 4)
            if beat % 2 == 1:
                unit_step(e_transposes, beat - 1)
                unit_step(e_transposes, beat)
            unit_step(row_max, beat + 3)
            unit_step(exponential, beat + 1)
            if beat % 2 == 0:
                unit_step(copy_eT_pair, beat - 2)
            for job, args in side_jobs.get(beat, []):
                job(*args)
